import numpy as np
import ml_dtypes


def mxq(x, axis, fmt="e4m3"):
    dtype, down = {"e4m3": (ml_dtypes.float8_e4m3fn, 7), "e5m2": (ml_dtypes.float8_e5m2, 14)}[fmt]
    v = np.moveaxis(np.asarray(x, np.float32).astype(ml_dtypes.bfloat16).astype(np.float64), axis, -1)
    blocks = v.reshape(v.shape[:-1] + (-1, 32))
    amax = np.abs(blocks).max(-1, keepdims=True)
    byte = np.maximum(np.where(amax > 0, np.frexp(amax)[1] - 1 + 127, 0) - down, 1)
    scale = np.exp2(byte - 127.0)
    codes = (blocks / scale).astype(np.float32).astype(dtype).astype(np.float64)
    return np.moveaxis((codes * scale).reshape(v.shape), -1, axis)


WIDE = False


def mx_kscale(k):
    if not WIDE:
        return np.ones(k)
    levels = np.array([10, -10, 5, -5, 0])
    a = np.random.permutation(np.resize(levels, k // 512 * 4)).reshape(k // 512, 4)
    idx = np.arange(k)
    return np.exp2(a[idx // 512, idx % 128 // 32])


BF16 = ml_dtypes.bfloat16


def bf(x):
    return np.asarray(x, np.float32).astype(BF16)


def f64(x):
    return np.asarray(x).astype(np.float64)


NS, NT, DS, DT, DH, DB, DO, NF, SP = 1024, 4096, 1024, 128, 256, 1024, 512, 2, 32
EPS_ROW = 1e-8
EPS_BN = 1e-5


def row_norm(a):
    return a / np.maximum(a.sum(axis=1, keepdims=True), EPS_ROW)


def bn_eval(x, gamma, beta, mean, var):
    return (x - mean) * (gamma / np.sqrt(var + EPS_BN)) + beta


def setup_inputs():
    t = mx_kscale(DS)
    edges = np.random.random((NT, NS)) < 1.0 / SP
    linked = np.random.random((NT, 1)) > 0.03
    return {"H_source": bf(np.random.standard_normal((NS, DS)) * t),
            "A": bf(np.random.random((NT, NS)) * edges * linked),
            "W0": bf(np.random.standard_normal((DS, DH)) * np.sqrt(NS / SP / DS) / t[:, None]),
            "b0": bf(np.random.standard_normal(DH) * 0.1),
            "bn_gamma": bf(np.random.uniform(0.5, 1.5, DH)),
            "bn_beta": bf(np.random.standard_normal(DH) * 0.1),
            "bn_mean": bf(np.random.standard_normal(DH) * 0.1),
            "bn_var": bf(np.random.uniform(0.5, 1.5, DH))}


def reference(H_source, A, W0, b0, bn_gamma, bn_beta, bn_mean, bn_var):
    a_n = row_norm(f64(A))
    agg = mxq(a_n, 1, "e4m3") @ mxq(f64(H_source), 0, "e4m3")
    h = (mxq(agg, 1, "e4m3") @ mxq(f64(W0), 0, "e4m3")) + f64(b0)
    return np.maximum(bn_eval(h, f64(bn_gamma), f64(bn_beta), f64(bn_mean), f64(bn_var)), 0.0)

@@ -1,0 +1,258 @@
+from contextlib import ExitStack
+
+import concourse.masks as masks
+import concourse.mybir as mybir
+
+BF16 = mybir.dt.bfloat16
+F32 = mybir.dt.float32
+U32 = mybir.dt.uint32
+U8 = mybir.dt.uint8
+FP8X4 = mybir.dt.float8_e4m3fn_x4
+ALU = mybir.AluOpType
+FUNC = mybir.ActivationFunctionType
+
+P = 128
+PACK = 4
+K_PASS = P * PACK
+
+NT, NS, DS, DH = 4096, 1024, 1024, 256
+S_PASSES = NS // K_PASS
+D_PASSES = DS // K_PASS
+EPS_ROW = 1e-8
+EPS_BN = 1e-5
+
+UNIT_TILES = 2
+N_UNITS = NT // (UNIT_TILES * P)
+
+FLOPS = 2 * NT * NS * DS + 2 * NT * DS * DH
+
+
+def tile_bipartitegcnstack_pa_t_kernel(
+    tc, H_source, A, W0, b0, bn_gamma, bn_beta, bn_mean, bn_var, out
+):
+    nc = tc.nc
+
+    a_view = A.rearrange("(u p i) s -> u p i s", p=P, i=UNIT_TILES)
+    out_view = out.rearrange("(u p i) o -> u p i o", p=P, i=UNIT_TILES)
+    h_view = H_source.rearrange("(c p) d -> p c d", p=P)
+    w_view = W0.rearrange("(c p) o -> p c o", p=P)
+
+    with ExitStack() as ctx:
+        keep = ctx.enter_context(tc.tile_pool(name="keep", bufs=1))
+        a_pool = ctx.enter_context(tc.tile_pool(name="a_pool", bufs=N_UNITS))
+        work = ctx.enter_context(tc.tile_pool(name="work", bufs=3))
+        psum = ctx.enter_context(tc.psum_pool(name="psum", bufs=2))
+
+        a_raw = {}
+
+        def load_a(u):
+            a_raw[u] = a_pool.tile([P, UNIT_TILES, NS], BF16, name="a_raw")
+            nc.sync.dma_start(out=a_raw[u][:], in_=a_view[u])
+
+        h_raw = keep.tile([P, D_PASSES, S_PASSES * PACK, K_PASS], BF16)
+        w_raw = keep.tile([P, D_PASSES * PACK, DH], BF16)
+        vectors = {}
+
+        load_a(0)
+        nc.sync.dma_start(out=h_raw[:, 0], in_=h_view[:, :, 0:K_PASS])
+        nc.sync.dma_start(out=h_raw[:, 1], in_=h_view[:, :, K_PASS : 2 * K_PASS])
+        load_a(1)
+        nc.sync.dma_start(out=w_raw[:], in_=w_view)
+        load_a(2)
+        for name, vector in (
+            ("var", bn_var),
+            ("gamma", bn_gamma),
+            ("b0", b0),
+            ("mean", bn_mean),
+            ("beta", bn_beta),
+        ):
+            vectors[name] = keep.tile([P, DH], BF16, name="vec_" + name)
+            nc.sync.dma_start(out=vectors[name][:], in_=vector.partition_broadcast(P))
+        for u in range(3, N_UNITS):
+            load_a(u)
+
+        ident = keep.tile([P, P], BF16)
+        masks.make_identity(nc, ident[:])
+        one = keep.tile([P, 1], F32)
+        nc.vector.memset(one[:], 1.0)
+        nc.scalar.activation(out=one[:], in_=one[:], func=FUNC.Sqrt)
+
+        h_grp = keep.tile([P, D_PASSES, S_PASSES, K_PASS, PACK], BF16, align_bytes=64)
+        h_codes = keep.tile([P, D_PASSES, S_PASSES, K_PASS], U32, align_bytes=64)
+        h_scales = keep.tile([P, D_PASSES, S_PASSES, K_PASS], U8, align_bytes=64)
+        w_grp = keep.tile([P, D_PASSES, DH, PACK], BF16, align_bytes=64)
+        w_codes = keep.tile([P, D_PASSES, DH], U32, align_bytes=64)
+        w_scales = keep.tile([P, D_PASSES, DH], U8, align_bytes=64)
+
+        def side_by_side(dst, src):
+            nc.vector.tensor_copy(
+                out=dst.rearrange("p (c i) j -> p c j i", i=4),
+                in_=src.rearrange("p j (c i) -> p c j i", i=4),
+            )
+
+        def pack_h(half):
+            for g in range(S_PASSES):
+                side_by_side(h_grp[:, half, g], h_raw[:, half, PACK * g : PACK * (g + 1), :])
+            nc.vector.quantize_mx(
+                out=h_codes[:, half].rearrange("p g d -> p (g d)").bitcast(FP8X4),
+                scales=h_scales[:, half].rearrange("p g d -> p (g d)"),
+                in_=h_grp[:, half].rearrange("p g d j -> p (g d j)"),
+            )
+
+        def pack_w():
+            for g in range(D_PASSES):
+                side_by_side(w_grp[:, g], w_raw[:, PACK * g : PACK * (g + 1), :])
+            nc.vector.quantize_mx(
+                out=w_codes[:].rearrange("p g o -> p (g o)").bitcast(FP8X4),
+                scales=w_scales[:].rearrange("p g o -> p (g o)"),
+                in_=w_grp[:].rearrange("p g o j -> p (g o j)"),
+            )
+
+        bn_scale = keep.tile([P, DH], F32)
+        bn_shift = keep.tile([P, DH], F32)
+
+        def prepare_batch_norm():
+            nc.gpsimd.tensor_scalar(
+                out=bn_scale[:], in0=vectors["var"][:], scalar1=1.0, scalar2=EPS_BN,
+                op0=ALU.mult, op1=ALU.add,
+            )
+            nc.scalar.activation(out=bn_scale[:], in_=bn_scale[:], func=FUNC.Sqrt)
+            nc.vector.reciprocal(out=bn_scale[:], in_=bn_scale[:])
+            nc.gpsimd.tensor_tensor(
+                out=bn_scale[:], in0=bn_scale[:], in1=vectors["gamma"][:], op=ALU.mult
+            )
+            nc.gpsimd.tensor_tensor(
+                out=bn_shift[:], in0=vectors["b0"][:], in1=vectors["mean"][:], op=ALU.subtract
+            )
+            nc.gpsimd.tensor_tensor(out=bn_shift[:], in0=bn_shift[:], in1=bn_scale[:], op=ALU.mult)
+            nc.gpsimd.tensor_tensor(
+                out=bn_shift[:], in0=bn_shift[:], in1=vectors["beta"][:], op=ALU.add
+            )
+
+        unused = keep.tile([P, NS], BF16)
+        a_n, at_banks, at_codes, at_scales = {}, {}, {}, {}
+        agg_banks, agg_codes, agg_scales, h_banks = {}, {}, {}, {}
+
+        def normalise(u):
+            sums = work.tile([P, UNIT_TILES], F32, name="sums")
+            for i in range(UNIT_TILES):
+                nc.vector.tensor_scalar(
+                    out=unused[:], in0=a_raw[u][:, i, :], scalar1=1.0, scalar2=None,
+                    op0=ALU.mult, op1=ALU.add, accum_out=sums[:, i : i + 1],
+                )
+            nc.vector.tensor_scalar_max(out=sums[:], in0=sums[:], scalar1=EPS_ROW)
+            nc.vector.reciprocal(out=sums[:], in_=sums[:])
+            a_n[u] = work.tile([P, UNIT_TILES, NS], BF16, name="a_n")
+            for i in range(UNIT_TILES):
+                nc.vector.tensor_scalar(
+                    out=a_n[u][:, i, :], in0=a_raw[u][:, i, :], scalar1=sums[:, i : i + 1],
+                    scalar2=None, op0=ALU.mult,
+                )
+
+        def transpose(u):
+            at_banks[u] = []
+            for i in range(UNIT_TILES):
+                at_bank = psum.tile([P, S_PASSES * PACK, P], BF16, tag="at", bufs=2, name="at_bank")
+                for c in range(S_PASSES * PACK):
+                    nc.tensor.transpose(at_bank[:, c, :], a_n[u][:, i, P * c : P * (c + 1)], ident[:])
+                at_banks[u].append(at_bank)
+
+        def pack_a(u):
+            at_grp = work.tile([P, UNIT_TILES, S_PASSES, P, PACK], BF16, align_bytes=64, name="at_grp")
+            for i in range(UNIT_TILES):
+                nc.scalar.copy(
+                    out=at_grp[:, i], in_=at_banks[u][i][:].rearrange("p (g j) t -> p g t j", j=PACK)
+                )
+            at_codes[u] = work.tile([P, UNIT_TILES, S_PASSES, P], U32, align_bytes=64, name="at_codes")
+            at_scales[u] = work.tile([P, UNIT_TILES, S_PASSES, P], U8, align_bytes=64, name="at_scales")
+            nc.vector.quantize_mx(
+                out=at_codes[u][:].rearrange("p i g t -> p (i g t)").bitcast(FP8X4),
+                scales=at_scales[u][:].rearrange("p i g t -> p (i g t)"),
+                in_=at_grp[:].rearrange("p i g t j -> p (i g t j)"),
+            )
+
+        def aggregate(u):
+            agg_banks[u] = []
+            for i in range(UNIT_TILES):
+                for half in range(D_PASSES):
+                    agg_bank = psum.tile([P, PACK, P], F32, tag="agg", bufs=4, name="agg_bank")
+                    for j in range(PACK):
+                        d_cols = slice(P * j, P * (j + 1))
+                        for g in range(S_PASSES):
+                            nc.tensor.matmul_mx(
+                                out=agg_bank[:, j, :],
+                                lhsT=h_codes[:, half, g, d_cols].bitcast(FP8X4),
+                                lhsT_scale=h_scales[:, half, g, d_cols],
+                                rhs=at_codes[u][:, i, g, :].bitcast(FP8X4),
+                                rhs_scale=at_scales[u][:, i, g, :],
+                                start=(g == 0),
+                                stop=(g == S_PASSES - 1),
+                            )
+                    agg_banks[u].append(agg_bank)
+
+        def pack_agg(u):
+            agg_grp = work.tile([P, UNIT_TILES * D_PASSES, P, PACK], BF16, align_bytes=64, name="agg_grp")
+            for b in range(UNIT_TILES * D_PASSES):
+                nc.scalar.copy(out=agg_grp[:, b], in_=agg_banks[u][b][:].rearrange("p j t -> p t j"))
+            agg_codes[u] = work.tile([P, UNIT_TILES, D_PASSES, P], U32, align_bytes=64, name="agg_codes")
+            agg_scales[u] = work.tile([P, UNIT_TILES, D_PASSES, P], U8, align_bytes=64, name="agg_scales")
+            nc.vector.quantize_mx(
+                out=agg_codes[u][:].rearrange("p i g t -> p (i g t)").bitcast(FP8X4),
+                scales=agg_scales[u][:].rearrange("p i g t -> p (i g t)"),
+                in_=agg_grp[:].rearrange("p b t j -> p (b t j)"),
+            )
+
+        def project(u):
+            h_banks[u] = psum.tile([P, UNIT_TILES, DH], F32, tag="h", bufs=2, name="h_bank")
+            for i in range(UNIT_TILES):
+                for g in range(D_PASSES):
+                    nc.tensor.matmul_mx(
+                        out=h_banks[u][:, i, :],
+                        lhsT=agg_codes[u][:, i, g, :].bitcast(FP8X4),
+                        lhsT_scale=agg_scales[u][:, i, g, :],
+                        rhs=w_codes[:, g, :].bitcast(FP8X4),
+                        rhs_scale=w_scales[:, g, :],
+                        start=(g == 0),
+                        stop=(g == D_PASSES - 1),
+                    )
+
+        def finish(u):
+            both_tiles = [P, UNIT_TILES, DH]
+            y = work.tile(both_tiles, F32, name="y")
+            nc.vector.tensor_tensor(
+                out=y[:], in0=h_banks[u][:], in1=bn_scale[:].unsqueeze(1).to_broadcast(both_tiles),
+                op=ALU.mult,
+            )
+            nc.vector.tensor_tensor(
+                out=y[:], in0=y[:], in1=bn_shift[:].unsqueeze(1).to_broadcast(both_tiles), op=ALU.add
+            )
+            nc.vector.tensor_scalar_max(out=y[:], in0=y[:], scalar1=0.0)
+            nc.sync.dma_start(out=out_view[u], in_=y[:])
+
+        def step(k):
+            if k + 2 < N_UNITS:
+                normalise(k + 2)
+            if k + 1 < N_UNITS:
+                transpose(k + 1)
+            if k < N_UNITS:
+                aggregate(k)
+            if k + 1 < N_UNITS:
+                pack_a(k + 1)
+            if k >= 1:
+                project(k - 1)
+            if k < N_UNITS:
+                pack_agg(k)
+            if k >= 1:
+                finish(k - 1)
+
+        normalise(0)
+        pack_h(0)
+        transpose(0)
+        pack_a(0)
+        pack_h(1)
+        normalise(1)
+        pack_w()
+        step(0)
+        prepare_batch_norm()
+        for k in range(1, N_UNITS + 1):
+            step(k)

@@ -13,6 +13,7 @@ FUNC = mybir.ActivationFunctionType
 
 P = 128
 PACK = 4
+PAIR = 2
 K_PASS = P * PACK
 
 NT, NS, DS, DH = 4096, 1024, 1024, 256
@@ -34,7 +35,7 @@ def tile_bipartitegcnstack_pa_t_kernel(
 
     a_view = A.rearrange("(u p i) s -> u p i s", p=P, i=UNIT_TILES)
     out_view = out.rearrange("(u p i) o -> u p i o", p=P, i=UNIT_TILES)
-    h_view = H_source.rearrange("(c p) d -> p c d", p=P)
+    h_view = H_source.rearrange("(v p e) d -> v p e d", p=P, e=PAIR)
     w_view = W0.rearrange("(c p) o -> p c o", p=P)
 
     with ExitStack() as ctx:
@@ -49,13 +50,13 @@ def tile_bipartitegcnstack_pa_t_kernel(
             a_raw[u] = a_pool.tile([P, UNIT_TILES, NS], BF16, name="a_raw")
             nc.sync.dma_start(out=a_raw[u][:], in_=a_view[u])
 
-        h_raw = keep.tile([P, D_PASSES, S_PASSES * PACK, K_PASS], BF16)
+        h_raw = keep.tile([P, S_PASSES * PACK // PAIR, PAIR, DS], BF16)
         w_raw = keep.tile([P, D_PASSES * PACK, DH], BF16)
         vectors = {}
 
         load_a(0)
-        nc.sync.dma_start(out=h_raw[:, 0], in_=h_view[:, :, 0:K_PASS])
-        nc.sync.dma_start(out=h_raw[:, 1], in_=h_view[:, :, K_PASS : 2 * K_PASS])
+        for v in range(S_PASSES * PACK // PAIR):
+            nc.sync.dma_start(out=h_raw[:, v], in_=h_view[v])
         load_a(1)
         nc.sync.dma_start(out=w_raw[:], in_=w_view)
         load_a(2)
@@ -71,7 +72,7 @@ def tile_bipartitegcnstack_pa_t_kernel(
         for u in range(3, N_UNITS):
             load_a(u)
 
-        ident = keep.tile([P, P], BF16)
+        ident = keep.tile([P, P], F32)
         masks.make_identity(nc, ident[:])
         one = keep.tile([P, 1], F32)
         nc.vector.memset(one[:], 1.0)
@@ -84,15 +85,19 @@ def tile_bipartitegcnstack_pa_t_kernel(
         w_codes = keep.tile([P, D_PASSES, DH], U32, align_bytes=64)
         w_scales = keep.tile([P, D_PASSES, DH], U8, align_bytes=64)
 
-        def side_by_side(dst, src):
-            nc.vector.tensor_copy(
+        def side_by_side(dst, src, copy):
+            copy(
                 out=dst.rearrange("p (c i) j -> p c j i", i=4),
                 in_=src.rearrange("p j (c i) -> p c j i", i=4),
             )
 
-        def pack_h(half):
-            for g in range(S_PASSES):
-                side_by_side(h_grp[:, half, g], h_raw[:, half, PACK * g : PACK * (g + 1), :])
+        h_rows = h_raw[:].rearrange("p v e d -> p (v e) d")
+
+        def regroup_h(half, g, copy):
+            d_half = slice(K_PASS * half, K_PASS * (half + 1))
+            side_by_side(h_grp[:, half, g], h_rows[:, PACK * g : PACK * (g + 1), d_half], copy)
+
+        def quantise_h(half):
             nc.vector.quantize_mx(
                 out=h_codes[:, half].rearrange("p g d -> p (g d)").bitcast(FP8X4),
                 scales=h_scales[:, half].rearrange("p g d -> p (g d)"),
@@ -101,7 +106,7 @@ def tile_bipartitegcnstack_pa_t_kernel(
 
         def pack_w():
             for g in range(D_PASSES):
-                side_by_side(w_grp[:, g], w_raw[:, PACK * g : PACK * (g + 1), :])
+                side_by_side(w_grp[:, g], w_raw[:, PACK * g : PACK * (g + 1), :], nc.vector.tensor_copy)
             nc.vector.quantize_mx(
                 out=w_codes[:].rearrange("p g o -> p (g o)").bitcast(FP8X4),
                 scales=w_scales[:].rearrange("p g o -> p (g o)"),
@@ -130,76 +135,94 @@ def tile_bipartitegcnstack_pa_t_kernel(
             )
 
         unused = keep.tile([P, NS], BF16)
-        a_n, at_banks, at_codes, at_scales = {}, {}, {}, {}
-        agg_banks, agg_codes, agg_scales, h_banks = {}, {}, {}, {}
+        sums, a_n, at_banks, at_grp, at_codes, at_scales = {}, {}, {}, {}, {}, {}
+        agg_banks, agg_grp, agg_codes, agg_scales, h_banks, y = {}, {}, {}, {}, {}, {}
+        BANKS = [(i, half) for half in range(D_PASSES) for i in range(UNIT_TILES)]
 
-        def normalise(u):
-            sums = work.tile([P, UNIT_TILES], F32, name="sums")
+        def sum_rows(u):
+            sums[u] = work.tile([P, UNIT_TILES], F32, name="sums")
             for i in range(UNIT_TILES):
                 nc.vector.tensor_scalar(
                     out=unused[:], in0=a_raw[u][:, i, :], scalar1=1.0, scalar2=None,
-                    op0=ALU.mult, op1=ALU.add, accum_out=sums[:, i : i + 1],
+                    op0=ALU.mult, op1=ALU.add, accum_out=sums[u][:, i : i + 1],
                 )
-            nc.vector.tensor_scalar_max(out=sums[:], in0=sums[:], scalar1=EPS_ROW)
-            nc.vector.reciprocal(out=sums[:], in_=sums[:])
+
+        def clamp_sums(u):
+            nc.vector.tensor_scalar_max(out=sums[u][:], in0=sums[u][:], scalar1=EPS_ROW)
+
+        def invert_sums(u):
+            nc.vector.reciprocal(out=sums[u][:], in_=sums[u][:])
+
+        def normalise(u):
             a_n[u] = work.tile([P, UNIT_TILES, NS], BF16, name="a_n")
             for i in range(UNIT_TILES):
                 nc.vector.tensor_scalar(
-                    out=a_n[u][:, i, :], in0=a_raw[u][:, i, :], scalar1=sums[:, i : i + 1],
+                    out=a_n[u][:, i, :], in0=a_raw[u][:, i, :], scalar1=sums[u][:, i : i + 1],
                     scalar2=None, op0=ALU.mult,
                 )
 
         def transpose(u):
             at_banks[u] = []
             for i in range(UNIT_TILES):
-                at_bank = psum.tile([P, S_PASSES * PACK, P], BF16, tag="at", bufs=2, name="at_bank")
-                for c in range(S_PASSES * PACK):
-                    nc.tensor.transpose(at_bank[:, c, :], a_n[u][:, i, P * c : P * (c + 1)], ident[:])
+                at_bank = psum.tile([P, S_PASSES * PACK // PAIR, P], F32, tag="at", bufs=2, name="at_bank")
+                words = a_n[u][:, i, :].bitcast(F32)
+                for v in range(S_PASSES * PACK // PAIR):
+                    nc.tensor.transpose(at_bank[:, v, :], words[:, P * v : P * (v + 1)], ident[:])
                 at_banks[u].append(at_bank)
 
-        def pack_a(u):
-            at_grp = work.tile([P, UNIT_TILES, S_PASSES, P, PACK], BF16, align_bytes=64, name="at_grp")
+        def empty_at(u):
+            at_grp[u] = work.tile([P, UNIT_TILES, S_PASSES, P, PACK], BF16, align_bytes=64, name="at_grp")
             for i in range(UNIT_TILES):
                 nc.scalar.copy(
-                    out=at_grp[:, i], in_=at_banks[u][i][:].rearrange("p (g j) t -> p g t j", j=PACK)
+                    out=at_grp[u][:, i].rearrange("p g t j -> p (g t j)").bitcast(F32).rearrange(
+                        "p (g t h) -> p g t h", g=S_PASSES, h=PACK // PAIR
+                    ),
+                    in_=at_banks[u][i][:].rearrange("p (g h) t -> p g t h", h=PACK // PAIR),
                 )
+
+        def quantise_at(u):
             at_codes[u] = work.tile([P, UNIT_TILES, S_PASSES, P], U32, align_bytes=64, name="at_codes")
             at_scales[u] = work.tile([P, UNIT_TILES, S_PASSES, P], U8, align_bytes=64, name="at_scales")
             nc.vector.quantize_mx(
                 out=at_codes[u][:].rearrange("p i g t -> p (i g t)").bitcast(FP8X4),
                 scales=at_scales[u][:].rearrange("p i g t -> p (i g t)"),
-                in_=at_grp[:].rearrange("p i g t j -> p (i g t j)"),
+                in_=at_grp[u][:].rearrange("p i g t j -> p (i g t j)"),
             )
 
-        def aggregate(u):
-            agg_banks[u] = []
-            for i in range(UNIT_TILES):
-                for half in range(D_PASSES):
-                    agg_bank = psum.tile([P, PACK, P], F32, tag="agg", bufs=4, name="agg_bank")
-                    for j in range(PACK):
-                        d_cols = slice(P * j, P * (j + 1))
-                        for g in range(S_PASSES):
-                            nc.tensor.matmul_mx(
-                                out=agg_bank[:, j, :],
-                                lhsT=h_codes[:, half, g, d_cols].bitcast(FP8X4),
-                                lhsT_scale=h_scales[:, half, g, d_cols],
-                                rhs=at_codes[u][:, i, g, :].bitcast(FP8X4),
-                                rhs_scale=at_scales[u][:, i, g, :],
-                                start=(g == 0),
-                                stop=(g == S_PASSES - 1),
-                            )
-                    agg_banks[u].append(agg_bank)
+        def aggregate(u, b):
+            i, half = BANKS[b]
+            agg_bank = psum.tile([P, PACK, P], F32, tag="agg", bufs=4, name="agg_bank")
+            for j in range(PACK):
+                d_cols = slice(P * j, P * (j + 1))
+                for g in range(S_PASSES):
+                    nc.tensor.matmul_mx(
+                        out=agg_bank[:, j, :],
+                        lhsT=h_codes[:, half, g, d_cols].bitcast(FP8X4),
+                        lhsT_scale=h_scales[:, half, g, d_cols],
+                        rhs=at_codes[u][:, i, g, :].bitcast(FP8X4),
+                        rhs_scale=at_scales[u][:, i, g, :],
+                        start=(g == 0),
+                        stop=(g == S_PASSES - 1),
+                    )
+            agg_banks[u, b] = agg_bank
 
-        def pack_agg(u):
-            agg_grp = work.tile([P, UNIT_TILES * D_PASSES, P, PACK], BF16, align_bytes=64, name="agg_grp")
-            for b in range(UNIT_TILES * D_PASSES):
-                nc.scalar.copy(out=agg_grp[:, b], in_=agg_banks[u][b][:].rearrange("p j t -> p t j"))
+        def empty_agg(u, b):
+            if b == 0:
+                agg_grp[u] = work.tile(
+                    [P, UNIT_TILES, D_PASSES, P, PACK], BF16, align_bytes=64, name="agg_grp"
+                )
+            i, half = BANKS[b]
+            nc.scalar.copy(
+                out=agg_grp[u][:, i, half], in_=agg_banks[u, b][:].rearrange("p j t -> p t j")
+            )
+
+        def quantise_agg(u):
             agg_codes[u] = work.tile([P, UNIT_TILES, D_PASSES, P], U32, align_bytes=64, name="agg_codes")
             agg_scales[u] = work.tile([P, UNIT_TILES, D_PASSES, P], U8, align_bytes=64, name="agg_scales")
             nc.vector.quantize_mx(
                 out=agg_codes[u][:].rearrange("p i g t -> p (i g t)").bitcast(FP8X4),
                 scales=agg_scales[u][:].rearrange("p i g t -> p (i g t)"),
-                in_=agg_grp[:].rearrange("p b t j -> p (b t j)"),
+                in_=agg_grp[u][:].rearrange("p i g t j -> p (i g t j)"),
             )
 
         def project(u):
@@ -216,43 +239,86 @@ def tile_bipartitegcnstack_pa_t_kernel(
                         stop=(g == D_PASSES - 1),
                     )
 
-        def finish(u):
-            both_tiles = [P, UNIT_TILES, DH]
-            y = work.tile(both_tiles, F32, name="y")
+        both_tiles = [P, UNIT_TILES, DH]
+
+        def scale_out(u):
+            y[u] = work.tile(both_tiles, F32, name="y")
             nc.vector.tensor_tensor(
-                out=y[:], in0=h_banks[u][:], in1=bn_scale[:].unsqueeze(1).to_broadcast(both_tiles),
+                out=y[u][:], in0=h_banks[u][:], in1=bn_scale[:].unsqueeze(1).to_broadcast(both_tiles),
                 op=ALU.mult,
             )
+
+        def shift_out(u):
             nc.vector.tensor_tensor(
-                out=y[:], in0=y[:], in1=bn_shift[:].unsqueeze(1).to_broadcast(both_tiles), op=ALU.add
+                out=y[u][:], in0=y[u][:], in1=bn_shift[:].unsqueeze(1).to_broadcast(both_tiles), op=ALU.add
             )
-            nc.vector.tensor_scalar_max(out=y[:], in0=y[:], scalar1=0.0)
-            nc.sync.dma_start(out=out_view[u], in_=y[:])
+
+        def relu_and_store(u):
+            nc.scalar.activation(out=y[u][:], in_=y[u][:], func=FUNC.Relu)
+            nc.sync.dma_start(out=out_view[u], in_=y[u][:])
+
+        def valid(u):
+            return 0 <= u < N_UNITS
 
         def step(k):
-            if k + 2 < N_UNITS:
-                normalise(k + 2)
-            if k + 1 < N_UNITS:
+            if valid(k - 2):
+                scale_out(k - 2)
+            if k == 0:
+                aggregate(0, 0)
+                aggregate(0, 1)
+            if valid(k + 1):
                 transpose(k + 1)
-            if k < N_UNITS:
-                aggregate(k)
-            if k + 1 < N_UNITS:
-                pack_a(k + 1)
-            if k >= 1:
+            if valid(k + 2):
+                normalise(k + 2)
+            if valid(k - 1):
+                empty_agg(k - 1, 3)
+                quantise_agg(k - 1)
+            if valid(k - 3):
+                relu_and_store(k - 3)
+            if valid(k + 1):
+                empty_at(k + 1)
+            if valid(k + 3):
+                sum_rows(k + 3)
+            if valid(k - 2):
+                shift_out(k - 2)
+            if valid(k + 3):
+                clamp_sums(k + 3)
+            if valid(k + 1):
+                quantise_at(k + 1)
+            if valid(k + 3):
+                invert_sums(k + 3)
+            if valid(k):
+                for b in range(4):
+                    if k > 0 or b > 1:
+                        aggregate(k, b)
+                    if b < 3:
+                        empty_agg(k, b)
+            if valid(k - 1):
                 project(k - 1)
-            if k < N_UNITS:
-                pack_agg(k)
-            if k >= 1:
-                finish(k - 1)
 
-        normalise(0)
-        pack_h(0)
-        transpose(0)
-        pack_a(0)
-        pack_h(1)
-        normalise(1)
-        pack_w()
-        step(0)
-        prepare_batch_norm()
-        for k in range(1, N_UNITS + 1):
-            step(k)
+        with tc.manual_schedule():
+            sum_rows(0)
+            clamp_sums(0)
+            invert_sums(0)
+            normalise(0)
+            transpose(0)
+            empty_at(0)
+            regroup_h(0, 0, nc.vector.tensor_copy)
+            quantise_at(0)
+            regroup_h(0, 1, nc.vector.tensor_copy)
+            regroup_h(1, 0, nc.scalar.copy)
+            regroup_h(1, 1, nc.scalar.copy)
+            sum_rows(1)
+            quantise_h(0)
+            clamp_sums(1)
+            sum_rows(2)
+            invert_sums(1)
+            clamp_sums(2)
+            normalise(1)
+            quantise_h(1)
+            invert_sums(2)
+            step(0)
+            pack_w()
+            prepare_batch_norm()
+            for k in range(1, N_UNITS + 3):
+                step(k)

@@ -135,17 +135,22 @@ def tile_bipartitegcnstack_pa_t_kernel(
             )
 
         unused = keep.tile([P, NS], BF16)
+        unused_too = keep.tile([P, NS], BF16)
         sums, a_n, at_banks, at_grp, at_codes, at_scales = {}, {}, {}, {}, {}, {}
         agg_banks, agg_grp, agg_codes, agg_scales, h_banks, y = {}, {}, {}, {}, {}, {}
         BANKS = [(i, half) for half in range(D_PASSES) for i in range(UNIT_TILES)]
 
         def sum_rows(u):
             sums[u] = work.tile([P, UNIT_TILES], F32, name="sums")
-            for i in range(UNIT_TILES):
-                nc.vector.tensor_scalar(
-                    out=unused[:], in0=a_raw[u][:, i, :], scalar1=1.0, scalar2=None,
-                    op0=ALU.mult, op1=ALU.add, accum_out=sums[u][:, i : i + 1],
-                )
+            nc.vector.tensor_scalar(
+                out=unused[:], in0=a_raw[u][:, 0, :], scalar1=1.0, scalar2=None,
+                op0=ALU.mult, op1=ALU.add, accum_out=sums[u][:, 0:1],
+            )
+
+        def sum_rows_on_scalar(u):
+            nc.scalar.activation(
+                out=unused_too[:], in_=a_raw[u][:, 1, :], func=FUNC.Copy, accum_out=sums[u][:, 1:2]
+            )
 
         def clamp_sums(u):
             nc.vector.tensor_scalar_max(out=sums[u][:], in0=sums[u][:], scalar1=EPS_ROW)
@@ -254,7 +259,7 @@ def tile_bipartitegcnstack_pa_t_kernel(
             )
 
         def relu_and_store(u):
-            nc.scalar.activation(out=y[u][:], in_=y[u][:], func=FUNC.Relu)
+            nc.vector.tensor_scalar_max(out=y[u][:], in0=y[u][:], scalar1=0.0)
             nc.sync.dma_start(out=out_view[u], in_=y[u][:])
 
         def valid(u):
@@ -269,24 +274,25 @@ def tile_bipartitegcnstack_pa_t_kernel(
             if valid(k + 1):
                 transpose(k + 1)
             if valid(k + 2):
-                normalise(k + 2)
+                invert_sums(k + 2)
             if valid(k - 1):
                 empty_agg(k - 1, 3)
                 quantise_agg(k - 1)
-            if valid(k - 3):
-                relu_and_store(k - 3)
+            if valid(k + 2):
+                normalise(k + 2)
             if valid(k + 1):
                 empty_at(k + 1)
             if valid(k + 3):
                 sum_rows(k + 3)
+                sum_rows_on_scalar(k + 3)
             if valid(k - 2):
                 shift_out(k - 2)
-            if valid(k + 3):
-                clamp_sums(k + 3)
             if valid(k + 1):
                 quantise_at(k + 1)
+            if valid(k - 2):
+                relu_and_store(k - 2)
             if valid(k + 3):
-                invert_sums(k + 3)
+                clamp_sums(k + 3)
             if valid(k):
                 for b in range(4):
                     if k > 0 or b > 1:
@@ -298,6 +304,7 @@ def tile_bipartitegcnstack_pa_t_kernel(
 
         with tc.manual_schedule():
             sum_rows(0)
+            sum_rows_on_scalar(0)
             clamp_sums(0)
             invert_sums(0)
             normalise(0)
@@ -309,16 +316,17 @@ def tile_bipartitegcnstack_pa_t_kernel(
             regroup_h(1, 0, nc.scalar.copy)
             regroup_h(1, 1, nc.scalar.copy)
             sum_rows(1)
+            sum_rows_on_scalar(1)
             quantise_h(0)
             clamp_sums(1)
             sum_rows(2)
+            sum_rows_on_scalar(2)
             invert_sums(1)
             clamp_sums(2)
             normalise(1)
             quantise_h(1)
-            invert_sums(2)
             step(0)
             pack_w()
             prepare_batch_norm()
-            for k in range(1, N_UNITS + 3):
+            for k in range(1, N_UNITS + 2):
                 step(k)

@@ -24,6 +24,7 @@ EPS_BN = 1e-5
 
 UNIT_TILES = 2
 N_UNITS = NT // (UNIT_TILES * P)
+BOTH = range(UNIT_TILES)
 
 FLOPS = 2 * NT * NS * DS + 2 * NT * DS * DH
 
@@ -46,17 +47,26 @@ def tile_bipartitegcnstack_pa_t_kernel(
 
         a_raw = {}
 
-        def load_a(u):
-            a_raw[u] = a_pool.tile([P, UNIT_TILES, NS], BF16, name="a_raw")
-            nc.sync.dma_start(out=a_raw[u][:], in_=a_view[u])
+        def load_a(u, tiles=BOTH):
+            if u not in a_raw:
+                a_raw[u] = a_pool.tile([P, UNIT_TILES, NS], BF16, name="a_raw")
+            cut = slice(tiles[0], tiles[-1] + 1)
+            nc.sync.dma_start(out=a_raw[u][:, cut], in_=a_view[u][:, cut])
 
-        h_raw = keep.tile([P, S_PASSES * PACK // PAIR, PAIR, DS], BF16)
+        h_raw = keep.tile([P, D_PASSES, S_PASSES * PACK // PAIR, PAIR, K_PASS], BF16)
+
+        def load_h(half):
+            for v in range(S_PASSES * PACK // PAIR):
+                nc.sync.dma_start(
+                    out=h_raw[:, half, v], in_=h_view[v, :, :, K_PASS * half : K_PASS * (half + 1)]
+                )
+
         w_raw = keep.tile([P, D_PASSES * PACK, DH], BF16)
         vectors = {}
 
         load_a(0)
-        for v in range(S_PASSES * PACK // PAIR):
-            nc.sync.dma_start(out=h_raw[:, v], in_=h_view[v])
+        load_h(0)
+        load_h(1)
         load_a(1)
         nc.sync.dma_start(out=w_raw[:], in_=w_view)
         load_a(2)
@@ -72,8 +82,10 @@ def tile_bipartitegcnstack_pa_t_kernel(
         for u in range(3, N_UNITS):
             load_a(u)
 
+        ident_bf16 = keep.tile([P, P], BF16)
+        masks.make_identity(nc, ident_bf16[:])
         ident = keep.tile([P, P], F32)
-        masks.make_identity(nc, ident[:])
+        nc.vector.tensor_copy(out=ident[:], in_=ident_bf16[:])
         one = keep.tile([P, 1], F32)
         nc.vector.memset(one[:], 1.0)
         nc.scalar.activation(out=one[:], in_=one[:], func=FUNC.Sqrt)
@@ -91,11 +103,10 @@ def tile_bipartitegcnstack_pa_t_kernel(
                 in_=src.rearrange("p j (c i) -> p c j i", i=4),
             )
 
-        h_rows = h_raw[:].rearrange("p v e d -> p (v e) d")
-
-        def regroup_h(half, g, copy):
-            d_half = slice(K_PASS * half, K_PASS * (half + 1))
-            side_by_side(h_grp[:, half, g], h_rows[:, PACK * g : PACK * (g + 1), d_half], copy)
+        def regroup_h(half, g, part, copy):
+            cols = slice(K_PASS // 2 * part, K_PASS // 2 * (part + 1))
+            rows = h_raw[:, half].rearrange("p v e d -> p (v e) d")
+            side_by_side(h_grp[:, half, g, cols], rows[:, PACK * g : PACK * (g + 1), cols], copy)
 
         def quantise_h(half):
             nc.vector.quantize_mx(
@@ -104,9 +115,10 @@ def tile_bipartitegcnstack_pa_t_kernel(
                 in_=h_grp[:, half].rearrange("p g d j -> p (g d j)"),
             )
 
-        def pack_w():
-            for g in range(D_PASSES):
-                side_by_side(w_grp[:, g], w_raw[:, PACK * g : PACK * (g + 1), :], nc.vector.tensor_copy)
+        def regroup_w(g, copy):
+            side_by_side(w_grp[:, g], w_raw[:, PACK * g : PACK * (g + 1), :], copy)
+
+        def quantise_w():
             nc.vector.quantize_mx(
                 out=w_codes[:].rearrange("p g o -> p (g o)").bitcast(FP8X4),
                 scales=w_scales[:].rearrange("p g o -> p (g o)"),
@@ -135,67 +147,117 @@ def tile_bipartitegcnstack_pa_t_kernel(
             )
 
         unused = keep.tile([P, NS], BF16)
-        unused_too = keep.tile([P, NS], BF16)
-        sums, a_n, at_banks, at_grp, at_codes, at_scales = {}, {}, {}, {}, {}, {}
-        agg_banks, agg_grp, agg_codes, agg_scales, h_banks, y = {}, {}, {}, {}, {}, {}
-        BANKS = [(i, half) for half in range(D_PASSES) for i in range(UNIT_TILES)]
+        unused_too = keep.tile([P, P], F32)
+        tiles_of = {}
 
-        def sum_rows(u):
-            sums[u] = work.tile([P, UNIT_TILES], F32, name="sums")
+        def unit_tile(pool, name, u, shape, dtype, **options):
+            if (name, u) not in tiles_of:
+                tiles_of[name, u] = pool.tile(shape, dtype, name=name, **options)
+            return tiles_of[name, u]
+
+        def sums_of(u):
+            return unit_tile(work, "sums", u, [P, UNIT_TILES], F32)
+
+        def a_n_of(u):
+            return unit_tile(work, "a_n", u, [P, UNIT_TILES, NS], BF16)
+
+        def folded_of(u):
+            return unit_tile(psum, "folded", u, [P, UNIT_TILES, P], F32, bufs=1)
+
+        def at_grp_of(u):
+            return unit_tile(
+                work, "at_grp", u, [P, UNIT_TILES, S_PASSES, P, PACK], BF16, align_bytes=64
+            )
+
+        def at_codes_of(u):
+            return unit_tile(work, "at_codes", u, [P, UNIT_TILES, S_PASSES, P], U32, align_bytes=64)
+
+        def at_scales_of(u):
+            return unit_tile(work, "at_scales", u, [P, UNIT_TILES, S_PASSES, P], U8, align_bytes=64)
+
+        def agg_grp_of(u):
+            return unit_tile(
+                work, "agg_grp", u, [P, UNIT_TILES, D_PASSES, P, PACK], BF16, align_bytes=64
+            )
+
+        def agg_codes_of(u):
+            return unit_tile(work, "agg_codes", u, [P, UNIT_TILES, D_PASSES, P], U32, align_bytes=64)
+
+        def agg_scales_of(u):
+            return unit_tile(work, "agg_scales", u, [P, UNIT_TILES, D_PASSES, P], U8, align_bytes=64)
+
+        def h_bank_of(u):
+            return unit_tile(psum, "h_bank", u, [P, UNIT_TILES, DH], F32, bufs=1)
+
+        def y_of(u):
+            return unit_tile(work, "y", u, [P, UNIT_TILES, DH], F32)
+
+        def span(tiles):
+            return slice(tiles[0], tiles[-1] + 1)
+
+        def sum_rows(u, i):
             nc.vector.tensor_scalar(
-                out=unused[:], in0=a_raw[u][:, 0, :], scalar1=1.0, scalar2=None,
-                op0=ALU.mult, op1=ALU.add, accum_out=sums[u][:, 0:1],
+                out=unused[:], in0=a_raw[u][:, i, :], scalar1=1.0, scalar2=None,
+                op0=ALU.mult, op1=ALU.add, accum_out=sums_of(u)[:, i : i + 1],
             )
 
-        def sum_rows_on_scalar(u):
+        def fold_rows(u, i):
+            for b in range(NS // P):
+                nc.tensor.matmul(
+                    out=folded_of(u)[:, i, :], lhsT=ident_bf16[:],
+                    rhs=a_raw[u][:, i, P * b : P * (b + 1)],
+                    start=(b == 0), stop=(b == NS // P - 1),
+                )
+
+        def sum_folded(u, i):
             nc.scalar.activation(
-                out=unused_too[:], in_=a_raw[u][:, 1, :], func=FUNC.Copy, accum_out=sums[u][:, 1:2]
+                out=unused_too[:], in_=folded_of(u)[:, i, :], func=FUNC.Copy,
+                accum_out=sums_of(u)[:, i : i + 1],
             )
 
-        def clamp_sums(u):
-            nc.vector.tensor_scalar_max(out=sums[u][:], in0=sums[u][:], scalar1=EPS_ROW)
+        def clamp_sums(u, tiles=BOTH):
+            part = sums_of(u)[:, span(tiles)]
+            nc.vector.tensor_scalar_max(out=part, in0=part, scalar1=EPS_ROW)
 
-        def invert_sums(u):
-            nc.vector.reciprocal(out=sums[u][:], in_=sums[u][:])
+        def invert_sums(u, tiles=BOTH):
+            part = sums_of(u)[:, span(tiles)]
+            nc.vector.reciprocal(out=part, in_=part)
 
-        def normalise(u):
-            a_n[u] = work.tile([P, UNIT_TILES, NS], BF16, name="a_n")
-            for i in range(UNIT_TILES):
+        def normalise(u, tiles=BOTH):
+            for i in tiles:
                 nc.vector.tensor_scalar(
-                    out=a_n[u][:, i, :], in0=a_raw[u][:, i, :], scalar1=sums[u][:, i : i + 1],
+                    out=a_n_of(u)[:, i, :], in0=a_raw[u][:, i, :], scalar1=sums_of(u)[:, i : i + 1],
                     scalar2=None, op0=ALU.mult,
                 )
 
-        def transpose(u):
-            at_banks[u] = []
-            for i in range(UNIT_TILES):
+        at_banks, agg_banks = {}, {}
+
+        def transpose(u, tiles=BOTH):
+            for i in tiles:
                 at_bank = psum.tile([P, S_PASSES * PACK // PAIR, P], F32, tag="at", bufs=2, name="at_bank")
-                words = a_n[u][:, i, :].bitcast(F32)
+                words = a_n_of(u)[:, i, :].bitcast(F32)
                 for v in range(S_PASSES * PACK // PAIR):
                     nc.tensor.transpose(at_bank[:, v, :], words[:, P * v : P * (v + 1)], ident[:])
-                at_banks[u].append(at_bank)
+                at_banks[u, i] = at_bank
 
-        def empty_at(u):
-            at_grp[u] = work.tile([P, UNIT_TILES, S_PASSES, P, PACK], BF16, align_bytes=64, name="at_grp")
-            for i in range(UNIT_TILES):
+        def empty_at(u, tiles=BOTH):
+            for i in tiles:
                 nc.scalar.copy(
-                    out=at_grp[u][:, i].rearrange("p g t j -> p (g t j)").bitcast(F32).rearrange(
+                    out=at_grp_of(u)[:, i].rearrange("p g t j -> p (g t j)").bitcast(F32).rearrange(
                         "p (g t h) -> p g t h", g=S_PASSES, h=PACK // PAIR
                     ),
-                    in_=at_banks[u][i][:].rearrange("p (g h) t -> p g t h", h=PACK // PAIR),
+                    in_=at_banks[u, i][:].rearrange("p (g h) t -> p g t h", h=PACK // PAIR),
                 )
 
-        def quantise_at(u):
-            at_codes[u] = work.tile([P, UNIT_TILES, S_PASSES, P], U32, align_bytes=64, name="at_codes")
-            at_scales[u] = work.tile([P, UNIT_TILES, S_PASSES, P], U8, align_bytes=64, name="at_scales")
+        def quantise_at(u, tiles=BOTH):
+            cut = span(tiles)
             nc.vector.quantize_mx(
-                out=at_codes[u][:].rearrange("p i g t -> p (i g t)").bitcast(FP8X4),
-                scales=at_scales[u][:].rearrange("p i g t -> p (i g t)"),
-                in_=at_grp[u][:].rearrange("p i g t j -> p (i g t j)"),
+                out=at_codes_of(u)[:, cut].rearrange("p i g t -> p (i g t)").bitcast(FP8X4),
+                scales=at_scales_of(u)[:, cut].rearrange("p i g t -> p (i g t)"),
+                in_=at_grp_of(u)[:, cut].rearrange("p i g t j -> p (i g t j)"),
             )
 
-        def aggregate(u, b):
-            i, half = BANKS[b]
+        def aggregate(u, i, half):
             agg_bank = psum.tile([P, PACK, P], F32, tag="agg", bufs=4, name="agg_bank")
             for j in range(PACK):
                 d_cols = slice(P * j, P * (j + 1))
@@ -204,129 +266,170 @@ def tile_bipartitegcnstack_pa_t_kernel(
                         out=agg_bank[:, j, :],
                         lhsT=h_codes[:, half, g, d_cols].bitcast(FP8X4),
                         lhsT_scale=h_scales[:, half, g, d_cols],
-                        rhs=at_codes[u][:, i, g, :].bitcast(FP8X4),
-                        rhs_scale=at_scales[u][:, i, g, :],
+                        rhs=at_codes_of(u)[:, i, g, :].bitcast(FP8X4),
+                        rhs_scale=at_scales_of(u)[:, i, g, :],
                         start=(g == 0),
                         stop=(g == S_PASSES - 1),
                     )
-            agg_banks[u, b] = agg_bank
+            agg_banks[u, i, half] = agg_bank
 
-        def empty_agg(u, b):
-            if b == 0:
-                agg_grp[u] = work.tile(
-                    [P, UNIT_TILES, D_PASSES, P, PACK], BF16, align_bytes=64, name="agg_grp"
-                )
-            i, half = BANKS[b]
-            nc.scalar.copy(
-                out=agg_grp[u][:, i, half], in_=agg_banks[u, b][:].rearrange("p j t -> p t j")
+        def empty_agg(u, i, half, copy=nc.scalar.copy):
+            copy(
+                out=agg_grp_of(u)[:, i, half],
+                in_=agg_banks[u, i, half][:].rearrange("p j t -> p t j"),
             )
 
-        def quantise_agg(u):
-            agg_codes[u] = work.tile([P, UNIT_TILES, D_PASSES, P], U32, align_bytes=64, name="agg_codes")
-            agg_scales[u] = work.tile([P, UNIT_TILES, D_PASSES, P], U8, align_bytes=64, name="agg_scales")
+        def quantise_agg(u, tiles=BOTH):
+            cut = span(tiles)
             nc.vector.quantize_mx(
-                out=agg_codes[u][:].rearrange("p i g t -> p (i g t)").bitcast(FP8X4),
-                scales=agg_scales[u][:].rearrange("p i g t -> p (i g t)"),
-                in_=agg_grp[u][:].rearrange("p i g t j -> p (i g t j)"),
+                out=agg_codes_of(u)[:, cut].rearrange("p i g t -> p (i g t)").bitcast(FP8X4),
+                scales=agg_scales_of(u)[:, cut].rearrange("p i g t -> p (i g t)"),
+                in_=agg_grp_of(u)[:, cut].rearrange("p i g t j -> p (i g t j)"),
             )
 
-        def project(u):
-            h_banks[u] = psum.tile([P, UNIT_TILES, DH], F32, tag="h", bufs=2, name="h_bank")
-            for i in range(UNIT_TILES):
+        def project(u, tiles=BOTH):
+            for i in tiles:
                 for g in range(D_PASSES):
                     nc.tensor.matmul_mx(
-                        out=h_banks[u][:, i, :],
-                        lhsT=agg_codes[u][:, i, g, :].bitcast(FP8X4),
-                        lhsT_scale=agg_scales[u][:, i, g, :],
+                        out=h_bank_of(u)[:, i, :],
+                        lhsT=agg_codes_of(u)[:, i, g, :].bitcast(FP8X4),
+                        lhsT_scale=agg_scales_of(u)[:, i, g, :],
                         rhs=w_codes[:, g, :].bitcast(FP8X4),
                         rhs_scale=w_scales[:, g, :],
                         start=(g == 0),
                         stop=(g == D_PASSES - 1),
                     )
 
-        both_tiles = [P, UNIT_TILES, DH]
-
-        def scale_out(u):
-            y[u] = work.tile(both_tiles, F32, name="y")
+        def scale_out(u, tiles=BOTH):
+            cut = span(tiles)
             nc.vector.tensor_tensor(
-                out=y[u][:], in0=h_banks[u][:], in1=bn_scale[:].unsqueeze(1).to_broadcast(both_tiles),
-                op=ALU.mult,
+                out=y_of(u)[:, cut], in0=h_bank_of(u)[:, cut],
+                in1=bn_scale[:].unsqueeze(1).to_broadcast([P, len(tiles), DH]), op=ALU.mult,
             )
 
-        def shift_out(u):
+        def shift_out(u, tiles=BOTH):
+            part = y_of(u)[:, span(tiles)]
             nc.vector.tensor_tensor(
-                out=y[u][:], in0=y[u][:], in1=bn_shift[:].unsqueeze(1).to_broadcast(both_tiles), op=ALU.add
+                out=part, in0=part, in1=bn_shift[:].unsqueeze(1).to_broadcast([P, len(tiles), DH]),
+                op=ALU.add,
             )
 
-        def relu_and_store(u):
-            nc.vector.tensor_scalar_max(out=y[u][:], in0=y[u][:], scalar1=0.0)
-            nc.sync.dma_start(out=out_view[u], in_=y[u][:])
+        def relu_and_store(u, tiles=BOTH):
+            cut = span(tiles)
+            part = y_of(u)[:, cut]
+            nc.scalar.activation(out=part, in_=part, func=FUNC.Relu)
+            nc.sync.dma_start(out=out_view[u][:, cut], in_=part)
+
+        BANKS = [(i, half) for i in BOTH for half in range(D_PASSES)]
+        LAST = N_UNITS - 1
 
         def valid(u):
             return 0 <= u < N_UNITS
 
+        def folds(u, i):
+            return u < 3 or i == 1
+
+        def take_sums(u):
+            for i in BOTH:
+                if folds(u, i):
+                    fold_rows(u, i)
+                    sum_folded(u, i)
+                else:
+                    sum_rows(u, i)
+
         def step(k):
             if valid(k - 2):
                 scale_out(k - 2)
-            if k == 0:
-                aggregate(0, 0)
-                aggregate(0, 1)
+            if k == 1:
+                aggregate(1, 0, 0)
+                aggregate(1, 0, 1)
             if valid(k + 1):
                 transpose(k + 1)
             if valid(k + 2):
                 invert_sums(k + 2)
-            if valid(k - 1):
-                empty_agg(k - 1, 3)
-                quantise_agg(k - 1)
+            empty_agg(k - 1, 1, 1)
+            quantise_agg(k - 1)
             if valid(k + 2):
                 normalise(k + 2)
+            if valid(k - 3):
+                relu_and_store(k - 3)
             if valid(k + 1):
                 empty_at(k + 1)
             if valid(k + 3):
-                sum_rows(k + 3)
-                sum_rows_on_scalar(k + 3)
+                take_sums(k + 3)
             if valid(k - 2):
                 shift_out(k - 2)
             if valid(k + 1):
                 quantise_at(k + 1)
-            if valid(k - 2):
-                relu_and_store(k - 2)
             if valid(k + 3):
                 clamp_sums(k + 3)
-            if valid(k):
-                for b in range(4):
-                    if k > 0 or b > 1:
-                        aggregate(k, b)
-                    if b < 3:
-                        empty_agg(k, b)
-            if valid(k - 1):
-                project(k - 1)
+            for i, half in BANKS:
+                if (k, i) != (1, 0):
+                    aggregate(k, i, half)
+                if (i, half) != BANKS[-1]:
+                    empty_agg(k, i, half)
+            project(k - 1)
 
+        on_vector, on_scalar = nc.vector.tensor_copy, nc.scalar.copy
         with tc.manual_schedule():
-            sum_rows(0)
-            sum_rows_on_scalar(0)
+            take_sums(0)
+            regroup_h(0, 0, 0, on_vector)
             clamp_sums(0)
+            regroup_h(0, 0, 1, on_vector)
             invert_sums(0)
+            regroup_h(0, 1, 1, on_scalar)
+            regroup_h(0, 1, 0, on_vector)
             normalise(0)
             transpose(0)
+            regroup_h(1, 0, 0, on_scalar)
             empty_at(0)
-            regroup_h(0, 0, nc.vector.tensor_copy)
-            quantise_at(0)
-            regroup_h(0, 1, nc.vector.tensor_copy)
-            regroup_h(1, 0, nc.scalar.copy)
-            regroup_h(1, 1, nc.scalar.copy)
-            sum_rows(1)
-            sum_rows_on_scalar(1)
             quantise_h(0)
-            clamp_sums(1)
-            sum_rows(2)
-            sum_rows_on_scalar(2)
-            invert_sums(1)
-            clamp_sums(2)
-            normalise(1)
+            regroup_h(1, 0, 1, on_scalar)
+            regroup_h(1, 1, 0, on_vector)
+            regroup_h(1, 1, 1, on_vector)
+            quantise_at(0)
+            take_sums(1)
+            aggregate(0, 0, 0)
+            aggregate(0, 1, 0)
             quantise_h(1)
-            step(0)
-            pack_w()
+            clamp_sums(1)
+            invert_sums(1)
+            normalise(1)
+            aggregate(0, 0, 1)
+            transpose(1, [0])
+            empty_agg(0, 0, 0)
+            empty_at(1, [0])
+            empty_agg(0, 1, 0)
+            aggregate(0, 1, 1)
+            transpose(1, [1])
+            quantise_at(1, [0])
+            empty_at(1, [1])
+            take_sums(2)
+            empty_agg(0, 0, 1)
+            regroup_w(0, on_vector)
+            quantise_at(1, [1])
+            clamp_sums(2)
+            regroup_w(1, on_vector)
+            invert_sums(2)
+            normalise(2)
+            take_sums(3)
+            quantise_w()
+            clamp_sums(3)
             prepare_batch_norm()
-            for k in range(1, N_UNITS + 2):
+            for k in range(1, N_UNITS):
                 step(k)
+            empty_agg(LAST, 1, 1)
+            quantise_agg(LAST, [0])
+            relu_and_store(LAST - 2)
+            scale_out(LAST - 1)
+            project(LAST, [0])
+            quantise_agg(LAST, [1])
+            project(LAST, [1])
+            shift_out(LAST - 1)
+            scale_out(LAST, [0])
+            relu_and_store(LAST - 1)
+            scale_out(LAST, [1])
+            shift_out(LAST, [0])
+            relu_and_store(LAST, [0])
+            shift_out(LAST, [1])
+            relu_and_store(LAST, [1])

@@ -66,10 +66,10 @@ def tile_bipartitegcnstack_pa_t_kernel(
 
         load_a(0)
         load_h(0)
-        load_h(1)
         load_a(1)
-        nc.sync.dma_start(out=w_raw[:], in_=w_view)
+        load_h(1)
         load_a(2)
+        nc.sync.dma_start(out=w_raw[:], in_=w_view)
         for name, vector in (
             ("var", bn_var),
             ("gamma", bn_gamma),
@@ -147,6 +147,7 @@ def tile_bipartitegcnstack_pa_t_kernel(
             )
 
         unused = keep.tile([P, NS], BF16)
+        unused_wide = keep.tile([P, NS], BF16)
         unused_too = keep.tile([P, P], F32)
         tiles_of = {}
 
@@ -212,6 +213,12 @@ def tile_bipartitegcnstack_pa_t_kernel(
         def sum_folded(u, i):
             nc.scalar.activation(
                 out=unused_too[:], in_=folded_of(u)[:, i, :], func=FUNC.Copy,
+                accum_out=sums_of(u)[:, i : i + 1],
+            )
+
+        def sum_rows_on_scalar(u, i):
+            nc.scalar.activation(
+                out=unused_wide[:], in_=a_raw[u][:, i, :], func=FUNC.Copy,
                 accum_out=sums_of(u)[:, i : i + 1],
             )
 
@@ -314,28 +321,33 @@ def tile_bipartitegcnstack_pa_t_kernel(
                 op=ALU.add,
             )
 
-        def relu_and_store(u, tiles=BOTH):
-            cut = span(tiles)
-            part = y_of(u)[:, cut]
-            nc.scalar.activation(out=part, in_=part, func=FUNC.Relu)
-            nc.sync.dma_start(out=out_view[u][:, cut], in_=part)
-
         BANKS = [(i, half) for i in BOTH for half in range(D_PASSES)]
         LAST = N_UNITS - 1
 
         def valid(u):
             return 0 <= u < N_UNITS
 
-        def folds(u, i):
-            return u < 3 or i == 1
+        def busy_tensor(u):
+            return u % 2 == 0
 
         def take_sums(u):
             for i in BOTH:
-                if folds(u, i):
+                if u < 3 or (i == 1 and busy_tensor(u)):
                     fold_rows(u, i)
                     sum_folded(u, i)
+                elif i == 1:
+                    sum_rows_on_scalar(u, i)
                 else:
                     sum_rows(u, i)
+
+        def relu_and_store(u, tiles=BOTH):
+            cut = span(tiles)
+            part = y_of(u)[:, cut]
+            if busy_tensor(u):
+                nc.scalar.activation(out=part, in_=part, func=FUNC.Relu)
+            else:
+                nc.vector.tensor_scalar_max(out=part, in0=part, scalar1=0.0)
+            nc.sync.dma_start(out=out_view[u][:, cut], in_=part)
 
         def step(k):
             if valid(k - 2):
@@ -380,37 +392,34 @@ def tile_bipartitegcnstack_pa_t_kernel(
             regroup_h(0, 1, 1, on_scalar)
             regroup_h(0, 1, 0, on_vector)
             normalise(0)
+            take_sums(1)
             transpose(0)
-            regroup_h(1, 0, 0, on_scalar)
             empty_at(0)
+            regroup_h(1, 0, 0, on_scalar)
             quantise_h(0)
-            regroup_h(1, 0, 1, on_scalar)
+            clamp_sums(1)
             regroup_h(1, 1, 0, on_vector)
+            invert_sums(1)
             regroup_h(1, 1, 1, on_vector)
             quantise_at(0)
-            take_sums(1)
+            normalise(1)
+            take_sums(2)
             aggregate(0, 0, 0)
             aggregate(0, 1, 0)
+            transpose(1)
+            empty_at(1)
+            regroup_h(1, 0, 1, on_vector)
             quantise_h(1)
-            clamp_sums(1)
-            invert_sums(1)
-            normalise(1)
-            aggregate(0, 0, 1)
-            transpose(1, [0])
-            empty_agg(0, 0, 0)
-            empty_at(1, [0])
-            empty_agg(0, 1, 0)
-            aggregate(0, 1, 1)
-            transpose(1, [1])
-            quantise_at(1, [0])
-            empty_at(1, [1])
-            take_sums(2)
-            empty_agg(0, 0, 1)
-            regroup_w(0, on_vector)
-            quantise_at(1, [1])
             clamp_sums(2)
-            regroup_w(1, on_vector)
+            empty_agg(0, 0, 0)
+            aggregate(0, 0, 1)
+            empty_agg(0, 1, 0)
+            quantise_at(1)
+            aggregate(0, 1, 1)
             invert_sums(2)
+            empty_agg(0, 0, 1)
+            for g in range(D_PASSES):
+                regroup_w(g, on_vector)
             normalise(2)
             take_sums(3)
             quantise_w()

@@ -53,13 +53,11 @@ def tile_bipartitegcnstack_pa_t_kernel(
             cut = slice(tiles[0], tiles[-1] + 1)
             nc.sync.dma_start(out=a_raw[u][:, cut], in_=a_view[u][:, cut])
 
-        h_raw = keep.tile([P, D_PASSES, S_PASSES * PACK // PAIR, PAIR, K_PASS], BF16)
+        h_raw = keep.tile([P, S_PASSES * PACK // PAIR, PAIR, DS], BF16)
 
-        def load_h(half):
-            for v in range(S_PASSES * PACK // PAIR):
-                nc.sync.dma_start(
-                    out=h_raw[:, half, v], in_=h_view[v, :, :, K_PASS * half : K_PASS * (half + 1)]
-                )
+        def load_h(g):
+            for v in range(PACK // PAIR * g, PACK // PAIR * (g + 1)):
+                nc.sync.dma_start(out=h_raw[:, v], in_=h_view[v])
 
         w_raw = keep.tile([P, D_PASSES * PACK, DH], BF16)
         vectors = {}
@@ -70,6 +68,8 @@ def tile_bipartitegcnstack_pa_t_kernel(
         load_h(1)
         load_a(2)
         nc.sync.dma_start(out=w_raw[:], in_=w_view)
+        for u in range(3, 6):
+            load_a(u)
         for name, vector in (
             ("var", bn_var),
             ("gamma", bn_gamma),
@@ -79,7 +79,7 @@ def tile_bipartitegcnstack_pa_t_kernel(
         ):
             vectors[name] = keep.tile([P, DH], BF16, name="vec_" + name)
             nc.sync.dma_start(out=vectors[name][:], in_=vector.partition_broadcast(P))
-        for u in range(3, N_UNITS):
+        for u in range(6, N_UNITS):
             load_a(u)
 
         ident_bf16 = keep.tile([P, P], BF16)
@@ -103,10 +103,12 @@ def tile_bipartitegcnstack_pa_t_kernel(
                 in_=src.rearrange("p j (c i) -> p c j i", i=4),
             )
 
+        h_rows = h_raw[:].rearrange("p v e d -> p (v e) d")
+
         def regroup_h(half, g, part, copy):
             cols = slice(K_PASS // 2 * part, K_PASS // 2 * (part + 1))
-            rows = h_raw[:, half].rearrange("p v e d -> p (v e) d")
-            side_by_side(h_grp[:, half, g, cols], rows[:, PACK * g : PACK * (g + 1), cols], copy)
+            d_cols = slice(K_PASS * half + cols.start, K_PASS * half + cols.stop)
+            side_by_side(h_grp[:, half, g, cols], h_rows[:, PACK * g : PACK * (g + 1), d_cols], copy)
 
         def quantise_h(half):
             nc.vector.quantize_mx(
@@ -385,30 +387,30 @@ def tile_bipartitegcnstack_pa_t_kernel(
         on_vector, on_scalar = nc.vector.tensor_copy, nc.scalar.copy
         with tc.manual_schedule():
             take_sums(0)
-            regroup_h(0, 0, 0, on_vector)
             clamp_sums(0)
-            regroup_h(0, 0, 1, on_vector)
+            regroup_h(0, 0, 0, on_vector)
             invert_sums(0)
-            regroup_h(0, 1, 1, on_scalar)
-            regroup_h(0, 1, 0, on_vector)
+            regroup_h(1, 0, 0, on_scalar)
+            regroup_h(0, 0, 1, on_vector)
             normalise(0)
             take_sums(1)
             transpose(0)
+            regroup_h(0, 1, 1, on_scalar)
             empty_at(0)
-            regroup_h(1, 0, 0, on_scalar)
-            quantise_h(0)
+            regroup_h(0, 1, 0, on_vector)
             clamp_sums(1)
-            regroup_h(1, 1, 0, on_vector)
+            regroup_h(1, 0, 1, on_vector)
+            quantise_h(0)
             invert_sums(1)
-            regroup_h(1, 1, 1, on_vector)
             quantise_at(0)
             normalise(1)
             take_sums(2)
             aggregate(0, 0, 0)
             aggregate(0, 1, 0)
+            regroup_h(1, 1, 0, on_scalar)
+            regroup_h(1, 1, 1, on_vector)
             transpose(1)
             empty_at(1)
-            regroup_h(1, 0, 1, on_vector)
             quantise_h(1)
             clamp_sums(2)
             empty_agg(0, 0, 0)

from contextlib import ExitStack

import concourse.masks as masks
import concourse.mybir as mybir

BF16 = mybir.dt.bfloat16
F32 = mybir.dt.float32
U32 = mybir.dt.uint32
U8 = mybir.dt.uint8
FP8X4 = mybir.dt.float8_e4m3fn_x4
ALU = mybir.AluOpType
FUNC = mybir.ActivationFunctionType

P = 128
PACK = 4
PAIR = 2
K_PASS = P * PACK

NT, NS, DS, DH = 4096, 1024, 1024, 256
S_PASSES = NS // K_PASS
D_PASSES = DS // K_PASS
EPS_ROW = 1e-8
EPS_BN = 1e-5

UNIT_TILES = 2
N_UNITS = NT // (UNIT_TILES * P)
BOTH = range(UNIT_TILES)

FLOPS = 2 * NT * NS * DS + 2 * NT * DS * DH


def tile_bipartitegcnstack_pa_t_kernel(
    tc, H_source, A, W0, b0, bn_gamma, bn_beta, bn_mean, bn_var, out
):
    nc = tc.nc

    a_view = A.rearrange("(u p i) s -> u p i s", p=P, i=UNIT_TILES)
    out_view = out.rearrange("(u p i) o -> u p i o", p=P, i=UNIT_TILES)
    h_view = H_source.rearrange("(v p e) d -> v p e d", p=P, e=PAIR)
    w_view = W0.rearrange("(c p) o -> p c o", p=P)

    with ExitStack() as ctx:
        keep = ctx.enter_context(tc.tile_pool(name="keep", bufs=1))
        a_pool = ctx.enter_context(tc.tile_pool(name="a_pool", bufs=N_UNITS))
        work = ctx.enter_context(tc.tile_pool(name="work", bufs=3))
        psum = ctx.enter_context(tc.psum_pool(name="psum", bufs=2))

        a_raw = {}

        def load_a(u, tiles=BOTH):
            if u not in a_raw:
                a_raw[u] = a_pool.tile([P, UNIT_TILES, NS], BF16, name="a_raw")
            cut = slice(tiles[0], tiles[-1] + 1)
            nc.sync.dma_start(out=a_raw[u][:, cut], in_=a_view[u][:, cut])

        h_raw = keep.tile([P, S_PASSES * PACK // PAIR, PAIR, DS], BF16)

        def load_h(g):
            for v in range(PACK // PAIR * g, PACK // PAIR * (g + 1)):
                nc.sync.dma_start(out=h_raw[:, v], in_=h_view[v])

        w_raw = keep.tile([P, D_PASSES * PACK, DH], BF16)
        vectors = {}

        load_a(0)
        load_h(0)
        load_a(1)
        load_h(1)
        load_a(2)
        nc.sync.dma_start(out=w_raw[:], in_=w_view)
        for u in range(3, 6):
            load_a(u)
        for name, vector in (
            ("var", bn_var),
            ("gamma", bn_gamma),
            ("b0", b0),
            ("mean", bn_mean),
            ("beta", bn_beta),
        ):
            vectors[name] = keep.tile([P, DH], BF16, name="vec_" + name)
            nc.sync.dma_start(out=vectors[name][:], in_=vector.partition_broadcast(P))
        for u in range(6, N_UNITS):
            load_a(u)

        ident_bf16 = keep.tile([P, P], BF16)
        masks.make_identity(nc, ident_bf16[:])
        ident = keep.tile([P, P], F32)
        nc.vector.tensor_copy(out=ident[:], in_=ident_bf16[:])
        one = keep.tile([P, 1], F32)
        nc.vector.memset(one[:], 1.0)
        nc.scalar.activation(out=one[:], in_=one[:], func=FUNC.Sqrt)

        h_grp = keep.tile([P, D_PASSES, S_PASSES, K_PASS, PACK], BF16, align_bytes=64)
        h_codes = keep.tile([P, D_PASSES, S_PASSES, K_PASS], U32, align_bytes=64)
        h_scales = keep.tile([P, D_PASSES, S_PASSES, K_PASS], U8, align_bytes=64)
        w_grp = keep.tile([P, D_PASSES, DH, PACK], BF16, align_bytes=64)
        w_codes = keep.tile([P, D_PASSES, DH], U32, align_bytes=64)
        w_scales = keep.tile([P, D_PASSES, DH], U8, align_bytes=64)

        def side_by_side(dst, src, copy):
            copy(
                out=dst.rearrange("p (c i) j -> p c j i", i=4),
                in_=src.rearrange("p j (c i) -> p c j i", i=4),
            )

        h_rows = h_raw[:].rearrange("p v e d -> p (v e) d")

        def regroup_h(half, g, part, copy):
            cols = slice(K_PASS // 2 * part, K_PASS // 2 * (part + 1))
            d_cols = slice(K_PASS * half + cols.start, K_PASS * half + cols.stop)
            side_by_side(h_grp[:, half, g, cols], h_rows[:, PACK * g : PACK * (g + 1), d_cols], copy)

        def quantise_h(half):
            nc.vector.quantize_mx(
                out=h_codes[:, half].rearrange("p g d -> p (g d)").bitcast(FP8X4),
                scales=h_scales[:, half].rearrange("p g d -> p (g d)"),
                in_=h_grp[:, half].rearrange("p g d j -> p (g d j)"),
            )

        def regroup_w(g, copy):
            side_by_side(w_grp[:, g], w_raw[:, PACK * g : PACK * (g + 1), :], copy)

        def quantise_w():
            nc.vector.quantize_mx(
                out=w_codes[:].rearrange("p g o -> p (g o)").bitcast(FP8X4),
                scales=w_scales[:].rearrange("p g o -> p (g o)"),
                in_=w_grp[:].rearrange("p g o j -> p (g o j)"),
            )

        bn_scale = keep.tile([P, DH], F32)
        bn_shift = keep.tile([P, DH], F32)

        def prepare_batch_norm():
            nc.gpsimd.tensor_scalar(
                out=bn_scale[:], in0=vectors["var"][:], scalar1=1.0, scalar2=EPS_BN,
                op0=ALU.mult, op1=ALU.add,
            )
            nc.scalar.activation(out=bn_scale[:], in_=bn_scale[:], func=FUNC.Sqrt)
            nc.vector.reciprocal(out=bn_scale[:], in_=bn_scale[:])
            nc.gpsimd.tensor_tensor(
                out=bn_scale[:], in0=bn_scale[:], in1=vectors["gamma"][:], op=ALU.mult
            )
            nc.gpsimd.tensor_tensor(
                out=bn_shift[:], in0=vectors["b0"][:], in1=vectors["mean"][:], op=ALU.subtract
            )
            nc.gpsimd.tensor_tensor(out=bn_shift[:], in0=bn_shift[:], in1=bn_scale[:], op=ALU.mult)
            nc.gpsimd.tensor_tensor(
                out=bn_shift[:], in0=bn_shift[:], in1=vectors["beta"][:], op=ALU.add
            )

        unused = keep.tile([P, NS], BF16)
        unused_wide = keep.tile([P, NS], BF16)
        unused_too = keep.tile([P, P], F32)
        tiles_of = {}

        def unit_tile(pool, name, u, shape, dtype, **options):
            if (name, u) not in tiles_of:
                tiles_of[name, u] = pool.tile(shape, dtype, name=name, **options)
            return tiles_of[name, u]

        def sums_of(u):
            return unit_tile(work, "sums", u, [P, UNIT_TILES], F32)

        def a_n_of(u):
            return unit_tile(work, "a_n", u, [P, UNIT_TILES, NS], BF16)

        def folded_of(u):
            return unit_tile(psum, "folded", u, [P, UNIT_TILES, P], F32, bufs=1)

        def at_grp_of(u):
            return unit_tile(
                work, "at_grp", u, [P, UNIT_TILES, S_PASSES, P, PACK], BF16, align_bytes=64
            )

        def at_codes_of(u):
            return unit_tile(work, "at_codes", u, [P, UNIT_TILES, S_PASSES, P], U32, align_bytes=64)

        def at_scales_of(u):
            return unit_tile(work, "at_scales", u, [P, UNIT_TILES, S_PASSES, P], U8, align_bytes=64)

        def agg_grp_of(u):
            return unit_tile(
                work, "agg_grp", u, [P, UNIT_TILES, D_PASSES, P, PACK], BF16, align_bytes=64
            )

        def agg_codes_of(u):
            return unit_tile(work, "agg_codes", u, [P, UNIT_TILES, D_PASSES, P], U32, align_bytes=64)

        def agg_scales_of(u):
            return unit_tile(work, "agg_scales", u, [P, UNIT_TILES, D_PASSES, P], U8, align_bytes=64)

        def h_bank_of(u):
            return unit_tile(psum, "h_bank", u, [P, UNIT_TILES, DH], F32, bufs=1)

        def y_of(u):
            return unit_tile(work, "y", u, [P, UNIT_TILES, DH], F32)

        def span(tiles):
            return slice(tiles[0], tiles[-1] + 1)

        def sum_rows(u, i):
            nc.vector.tensor_scalar(
                out=unused[:], in0=a_raw[u][:, i, :], scalar1=1.0, scalar2=None,
                op0=ALU.mult, op1=ALU.add, accum_out=sums_of(u)[:, i : i + 1],
            )

        def fold_rows(u, i):
            for b in range(NS // P):
                nc.tensor.matmul(
                    out=folded_of(u)[:, i, :], lhsT=ident_bf16[:],
                    rhs=a_raw[u][:, i, P * b : P * (b + 1)],
                    start=(b == 0), stop=(b == NS // P - 1),
                )

        def sum_folded(u, i):
            nc.scalar.activation(
                out=unused_too[:], in_=folded_of(u)[:, i, :], func=FUNC.Copy,
                accum_out=sums_of(u)[:, i : i + 1],
            )

        def sum_rows_on_scalar(u, i):
            nc.scalar.activation(
                out=unused_wide[:], in_=a_raw[u][:, i, :], func=FUNC.Copy,
                accum_out=sums_of(u)[:, i : i + 1],
            )

        def clamp_sums(u, tiles=BOTH):
            part = sums_of(u)[:, span(tiles)]
            nc.vector.tensor_scalar_max(out=part, in0=part, scalar1=EPS_ROW)

        def invert_sums(u, tiles=BOTH):
            part = sums_of(u)[:, span(tiles)]
            nc.vector.reciprocal(out=part, in_=part)

        def normalise(u, tiles=BOTH):
            for i in tiles:
                nc.vector.tensor_scalar(
                    out=a_n_of(u)[:, i, :], in0=a_raw[u][:, i, :], scalar1=sums_of(u)[:, i : i + 1],
                    scalar2=None, op0=ALU.mult,
                )

        at_banks, agg_banks = {}, {}

        def transpose(u, tiles=BOTH):
            for i in tiles:
                at_bank = psum.tile([P, S_PASSES * PACK // PAIR, P], F32, tag="at", bufs=2, name="at_bank")
                words = a_n_of(u)[:, i, :].bitcast(F32)
                for v in range(S_PASSES * PACK // PAIR):
                    nc.tensor.transpose(at_bank[:, v, :], words[:, P * v : P * (v + 1)], ident[:])
                at_banks[u, i] = at_bank

        def empty_at(u, tiles=BOTH):
            for i in tiles:
                nc.scalar.copy(
                    out=at_grp_of(u)[:, i].rearrange("p g t j -> p (g t j)").bitcast(F32).rearrange(
                        "p (g t h) -> p g t h", g=S_PASSES, h=PACK // PAIR
                    ),
                    in_=at_banks[u, i][:].rearrange("p (g h) t -> p g t h", h=PACK // PAIR),
                )

        def quantise_at(u, tiles=BOTH):
            cut = span(tiles)
            nc.vector.quantize_mx(
                out=at_codes_of(u)[:, cut].rearrange("p i g t -> p (i g t)").bitcast(FP8X4),
                scales=at_scales_of(u)[:, cut].rearrange("p i g t -> p (i g t)"),
                in_=at_grp_of(u)[:, cut].rearrange("p i g t j -> p (i g t j)"),
            )

        def aggregate(u, i, half):
            agg_bank = psum.tile([P, PACK, P], F32, tag="agg", bufs=4, name="agg_bank")
            for j in range(PACK):
                d_cols = slice(P * j, P * (j + 1))
                for g in range(S_PASSES):
                    nc.tensor.matmul_mx(
                        out=agg_bank[:, j, :],
                        lhsT=h_codes[:, half, g, d_cols].bitcast(FP8X4),
                        lhsT_scale=h_scales[:, half, g, d_cols],
                        rhs=at_codes_of(u)[:, i, g, :].bitcast(FP8X4),
                        rhs_scale=at_scales_of(u)[:, i, g, :],
                        start=(g == 0),
                        stop=(g == S_PASSES - 1),
                    )
            agg_banks[u, i, half] = agg_bank

        def empty_agg(u, i, half, copy=nc.scalar.copy):
            copy(
                out=agg_grp_of(u)[:, i, half],
                in_=agg_banks[u, i, half][:].rearrange("p j t -> p t j"),
            )

        def quantise_agg(u, tiles=BOTH):
            cut = span(tiles)
            nc.vector.quantize_mx(
                out=agg_codes_of(u)[:, cut].rearrange("p i g t -> p (i g t)").bitcast(FP8X4),
                scales=agg_scales_of(u)[:, cut].rearrange("p i g t -> p (i g t)"),
                in_=agg_grp_of(u)[:, cut].rearrange("p i g t j -> p (i g t j)"),
            )

        def project(u, tiles=BOTH):
            for i in tiles:
                for g in range(D_PASSES):
                    nc.tensor.matmul_mx(
                        out=h_bank_of(u)[:, i, :],
                        lhsT=agg_codes_of(u)[:, i, g, :].bitcast(FP8X4),
                        lhsT_scale=agg_scales_of(u)[:, i, g, :],
                        rhs=w_codes[:, g, :].bitcast(FP8X4),
                        rhs_scale=w_scales[:, g, :],
                        start=(g == 0),
                        stop=(g == D_PASSES - 1),
                    )

        def scale_out(u, tiles=BOTH):
            cut = span(tiles)
            nc.vector.tensor_tensor(
                out=y_of(u)[:, cut], in0=h_bank_of(u)[:, cut],
                in1=bn_scale[:].unsqueeze(1).to_broadcast([P, len(tiles), DH]), op=ALU.mult,
            )

        def shift_out(u, tiles=BOTH):
            part = y_of(u)[:, span(tiles)]
            nc.vector.tensor_tensor(
                out=part, in0=part, in1=bn_shift[:].unsqueeze(1).to_broadcast([P, len(tiles), DH]),
                op=ALU.add,
            )

        BANKS = [(i, half) for i in BOTH for half in range(D_PASSES)]
        LAST = N_UNITS - 1

        def valid(u):
            return 0 <= u < N_UNITS

        def busy_tensor(u):
            return u % 2 == 0

        def take_sums(u):
            for i in BOTH:
                if u < 3 or (i == 1 and busy_tensor(u)):
                    fold_rows(u, i)
                    sum_folded(u, i)
                elif i == 1:
                    sum_rows_on_scalar(u, i)
                else:
                    sum_rows(u, i)

        def relu_and_store(u, tiles=BOTH):
            cut = span(tiles)
            part = y_of(u)[:, cut]
            if busy_tensor(u):
                nc.scalar.activation(out=part, in_=part, func=FUNC.Relu)
            else:
                nc.vector.tensor_scalar_max(out=part, in0=part, scalar1=0.0)
            nc.sync.dma_start(out=out_view[u][:, cut], in_=part)

        def step(k):
            if valid(k - 2):
                scale_out(k - 2)
            if k == 1:
                aggregate(1, 0, 0)
                aggregate(1, 0, 1)
            if valid(k + 1):
                transpose(k + 1)
            if valid(k + 2):
                invert_sums(k + 2)
            empty_agg(k - 1, 1, 1)
            quantise_agg(k - 1)
            if valid(k + 2):
                normalise(k + 2)
            if valid(k - 3):
                relu_and_store(k - 3)
            if valid(k + 1):
                empty_at(k + 1)
            if valid(k + 3):
                take_sums(k + 3)
            if valid(k - 2):
                shift_out(k - 2)
            if valid(k + 1):
                quantise_at(k + 1)
            if valid(k + 3):
                clamp_sums(k + 3)
            for i, half in BANKS:
                if (k, i) != (1, 0):
                    aggregate(k, i, half)
                if (i, half) != BANKS[-1]:
                    empty_agg(k, i, half)
            project(k - 1)

        on_vector, on_scalar = nc.vector.tensor_copy, nc.scalar.copy
        with tc.manual_schedule():
            take_sums(0)
            clamp_sums(0)
            regroup_h(0, 0, 0, on_vector)
            invert_sums(0)
            regroup_h(1, 0, 0, on_scalar)
            regroup_h(0, 0, 1, on_vector)
            normalise(0)
            take_sums(1)
            transpose(0)
            regroup_h(0, 1, 1, on_scalar)
            empty_at(0)
            regroup_h(0, 1, 0, on_vector)
            clamp_sums(1)
            regroup_h(1, 0, 1, on_vector)
            quantise_h(0)
            invert_sums(1)
            quantise_at(0)
            normalise(1)
            take_sums(2)
            aggregate(0, 0, 0)
            aggregate(0, 1, 0)
            regroup_h(1, 1, 0, on_scalar)
            regroup_h(1, 1, 1, on_vector)
            transpose(1)
            empty_at(1)
            quantise_h(1)
            clamp_sums(2)
            empty_agg(0, 0, 0)
            aggregate(0, 0, 1)
            empty_agg(0, 1, 0)
            quantise_at(1)
            aggregate(0, 1, 1)
            invert_sums(2)
            empty_agg(0, 0, 1)
            for g in range(D_PASSES):
                regroup_w(g, on_vector)
            normalise(2)
            take_sums(3)
            quantise_w()
            clamp_sums(3)
            prepare_batch_norm()
            for k in range(1, N_UNITS):
                step(k)
            empty_agg(LAST, 1, 1)
            quantise_agg(LAST, [0])
            relu_and_store(LAST - 2)
            scale_out(LAST - 1)
            project(LAST, [0])
            quantise_agg(LAST, [1])
            project(LAST, [1])
            shift_out(LAST - 1)
            scale_out(LAST, [0])
            relu_and_store(LAST - 1)
            scale_out(LAST, [1])
            shift_out(LAST, [0])
            relu_and_store(LAST, [0])
            shift_out(LAST, [1])
            relu_and_store(LAST, [1])
